import numpy as np
import ml_dtypes


def mxq(x, axis, fmt="e4m3"):
    dtype, down = {"e4m3": (ml_dtypes.float8_e4m3fn, 7), "e5m2": (ml_dtypes.float8_e5m2, 14)}[fmt]
    v = np.moveaxis(np.asarray(x, np.float32).astype(ml_dtypes.bfloat16).astype(np.float64), axis, -1)
    blocks = v.reshape(v.shape[:-1] + (-1, 32))
    amax = np.abs(blocks).max(-1, keepdims=True)
    byte = np.maximum(np.where(amax > 0, np.frexp(amax)[1] - 1 + 127, 0) - down, 1)
    scale = np.exp2(byte - 127.0)
    codes = (blocks / scale).astype(np.float32).astype(dtype).astype(np.float64)
    return np.moveaxis((codes * scale).reshape(v.shape), -1, axis)


WIDE = False


def mx_kscale(k):
    if not WIDE:
        return np.ones(k)
    levels = np.array([30, -30])
    if k % 512:
        return np.exp2(np.random.permutation(np.resize(levels, k // 32))).repeat(32)
    a = np.empty((k // 512, 16))
    for p in range(k // 512):
        a[p, :8] = np.random.permutation(np.resize(levels, 8))
        for g in range(8):
            far = levels[np.abs(levels - a[p, g]) >= 10]
            a[p, g + 8] = far[np.random.randint(len(far))]
    return np.exp2(a.ravel()).repeat(32)


BF16 = ml_dtypes.bfloat16


def bf(x):
    return np.asarray(x, np.float32).astype(BF16)


def f64(x):
    return np.asarray(x).astype(np.float64)


E2M1 = np.array([0.0, 0.5, 1.0, 1.5, 2.0, 3.0, 4.0, 6.0, -0.0, -0.5, -1.0, -1.5, -2.0, -3.0, -4.0, -6.0])


def pack_weight(w, fmt):
    k, n = w.shape
    w = f64(bf(w)).reshape(k // 32, 32, n)
    amax = np.abs(w).max(1)
    if fmt == "e4m3":
        byte = np.frexp(amax)[1] - 1 + 127 - 7
    else:
        mant, ex = np.frexp(amax / 6.0)
        byte = np.where(mant > 0.5, ex, ex - 1) + 127
    byte = np.clip(np.where(amax > 0, byte, 1), 1, 254)
    scaled = (w * np.exp2(127.0 - byte)[:, None, :]).reshape(k, n).astype(np.float32)
    by_word = np.ascontiguousarray(scaled.reshape(k // 512, 128, 4, n).transpose(0, 1, 3, 2))
    if fmt == "e4m3":
        words = by_word.astype(ml_dtypes.float8_e4m3fn).view(np.uint8)
    else:
        c = by_word.astype(ml_dtypes.float4_e2m1fn).view(np.uint8) & 0xF
        words = c[..., 0::2] | (c[..., 1::2] << 4)
    return np.ascontiguousarray(words), np.ascontiguousarray(byte.astype(np.uint8).reshape(k // 512, 16, n))


def unpack_weight(words, scales, fmt):
    g, p, n, _ = words.shape
    if fmt == "e4m3":
        vals = np.ascontiguousarray(words).view(ml_dtypes.float8_e4m3fn).astype(np.float64)
    else:
        nib = np.empty((g, p, n, 4), np.uint8)
        nib[..., 0::2] = words & 0xF
        nib[..., 1::2] = words >> 4
        vals = E2M1[nib]
    vals = vals * np.repeat(np.exp2(scales.astype(np.float64) - 127.0), 8, axis=1)[..., None]
    return vals.transpose(0, 1, 3, 2).reshape(g * 512, n)

def pack4(w):
    words, scales = pack_weight(w, "e2m1")
    return words.reshape(words.shape[0], 128, -1), scales


def unpack4(words, scales):
    return unpack_weight(words.reshape(words.shape[0], 128, -1, 2), scales, "e2m1")


B, T, C, H, G = 2, 512, 1024, 16, 16
HS = C // H
TG = T // G
THETA = 10000.0


def apply_rope(t, cos, sin):
    tp = t.reshape(B, T, H, HS // 2, 2)
    a, b = tp[..., 0], tp[..., 1]
    c = cos[None, :, None, :]
    s = sin[None, :, None, :]
    return np.stack([a * c - b * s, a * s + b * c], axis=-1).reshape(B, T, H, HS)


def grp(t):
    return t.reshape(B, G, TG, H, HS).transpose(0, 3, 1, 2, 4)


def with_summary(t):
    return np.concatenate([t, t.mean(axis=3, keepdims=True)], axis=3)


def setup_inputs():
    s = mx_kscale(C)
    x = np.random.standard_normal((B, T, C)) * 0.7 + np.random.standard_normal((B, 1, C)) * 0.7
    w = np.random.standard_normal((3 * C, C)) / np.sqrt(C)
    ang = np.arange(T)[:, None] / THETA ** (np.arange(0, HS, 2) / HS)[None, :]
    words, scales = pack4((w / s[None, :]).T)
    return {"x": bf(x * s), "w_attn_words": words, "w_attn_scales": scales, "freqs_cos": bf(np.cos(ang)), "freqs_sin": bf(np.sin(ang))}


def reference(x, w_attn_words, w_attn_scales, freqs_cos, freqs_sin):
    cos, sin = f64(freqs_cos), f64(freqs_sin)
    qkv = mxq(f64(x), 2, "e5m2") @ unpack4(w_attn_words, w_attn_scales)
    q, k, v = np.split(qkv, 3, axis=2)
    q = apply_rope(q.reshape(B, T, H, HS), cos, sin).reshape(B, T, C)
    k = apply_rope(k.reshape(B, T, H, HS), cos, sin).reshape(B, T, C)
    q, k, v = grp(q), grp(k), grp(v)
    return with_summary(q), with_summary(k), with_summary(v)

@@ -1,0 +1,296 @@
+from contextlib import ExitStack
+
+import concourse.mybir as mybir
+from concourse.masks import make_identity
+
+B, T, C, H, G = 2, 512, 1024, 16, 16
+HS = C // H
+TG = T // G
+FLOPS = 2 * B * T * C * 3 * C
+
+F32 = mybir.dt.float32
+BF16 = mybir.dt.bfloat16
+I32 = mybir.dt.int32
+U32 = mybir.dt.uint32
+U8 = mybir.dt.uint8
+E5M2X4 = mybir.dt.float8_e5m2_x4
+E2M1X4 = mybir.dt.float4_e2m1fn_x4
+ALU = mybir.AluOpType
+ACT = mybir.ActivationFunctionType
+
+P = 128
+SLOTS = B * T // P
+PAIRS = SLOTS // 2
+QUARTERS = TG // SLOTS
+PASSES = C // 512
+NCOL = 512
+CH = NCOL // HS
+Q0, Q1, K0, K1, V0, V1 = range(6)
+ROPE_ORDER = (K1, Q0, Q1, K0)
+
+
+def tile_causalselfattention2_pa_kernel(
+    tc, x, w_attn_words, w_attn_scales, freqs_cos, freqs_sin, out_0, out_1, out_2
+):
+    nc = tc.nc
+    outs = (out_0, out_1, out_2)
+
+    with ExitStack() as ctx:
+        keep = ctx.enter_context(tc.tile_pool(name="keep", bufs=1))
+        stage = ctx.enter_context(tc.tile_pool(name="stage", bufs=3))
+        psum = ctx.enter_context(tc.psum_pool(name="psum", bufs=1))
+        ctx.enter_context(tc.manual_schedule())
+
+        def bank(n):
+            return psum.tile([P, NCOL], F32, name="bank%d" % n)
+
+        x_sb = [keep.tile([P, C], BF16, name="x%d" % j) for j in range(SLOTS)]
+        x_view = x.rearrange("b (m j) c -> m b j c", j=SLOTS)
+        words = [keep.tile([P, PASSES, 2 * NCOL], U8, name="w%d" % c, align_bytes=64) for c in range(6)]
+        spans = ((K1, V1), (Q0, K1), (V1, V1 + 1))
+        planes = [
+            keep.tile([P, PASSES, (hi - lo) * NCOL], U8, name="plane%d" % lo, align_bytes=64) for lo, hi in spans
+        ]
+
+        def w_scale(c, g):
+            for (lo, hi), plane in zip(spans, planes):
+                if lo <= c < hi:
+                    return plane[:, g, (c - lo) * NCOL : (c - lo + 1) * NCOL]
+
+        def load_x(j):
+            nc.sync.dma_start(out=x_sb[j][:], in_=x_view[:, :, j, :])
+
+        def load_words(c):
+            src = w_attn_words[:, :, 2 * NCOL * c : 2 * NCOL * (c + 1)].rearrange("g p n -> p g n")
+            nc.sync.dma_start(out=words[c][:].bitcast(I32), in_=src.bitcast(I32))
+
+        def load_scales(n):
+            lo, hi = spans[n]
+            for quad in range(4):
+                src = w_attn_scales[:, 4 * quad : 4 * quad + 4, lo * NCOL : hi * NCOL].rearrange("g r n -> r g n")
+                nc.sync.dma_start(out=planes[n][32 * quad : 32 * quad + 4, :, :].bitcast(I32), in_=src.bitcast(I32))
+
+        for plane in planes:
+            nc.vector.memset(plane[:].bitcast(I32), 0)
+
+        load_x(0)
+        load_x(1)
+        load_scales(0)
+        load_words(K1)
+        load_words(V0)
+        for j in range(2, SLOTS):
+            load_x(j)
+        load_scales(1)
+        load_scales(2)
+        for c in (Q0, V1, Q1, K0):
+            load_words(c)
+
+        ident = keep.tile([P, P], F32)
+        make_identity(nc, ident[:])
+        cos_sb = keep.tile([P, SLOTS * HS // 2], BF16)
+        sin_sb = keep.tile([P, SLOTS * HS // 2], BF16)
+        for dst, src in ((cos_sb, freqs_cos), (sin_sb, freqs_sin)):
+            rows = src.rearrange("(m j) i -> m (j i)", j=SLOTS)
+            nc.gpsimd.dma_start(out=dst[:], in_=rows.unsqueeze(1).broadcast_to([P // B, B, SLOTS * HS // 2]))
+        fold = keep.tile([P, HS], F32)
+        nc.gpsimd.tensor_tensor(out=fold[:], in0=ident[:, 0:HS], in1=ident[:, HS:P], op=ALU.add)
+        signs = keep.tile([P, 2, 2], F32)
+        nc.gpsimd.memset(signs[:], 1.0)
+        nc.gpsimd.memset(signs[:, 1, 0:1], -1.0)
+        cos_tab = keep.tile([P, SLOTS * HS // 2, 2], F32)
+        sin_tab = keep.tile([P, SLOTS * HS // 2, 2], F32)
+        for n, (tab, src) in enumerate(((cos_tab, cos_sb), (sin_tab, sin_sb))):
+            nc.gpsimd.tensor_tensor(
+                out=tab[:],
+                in0=src[:].unsqueeze(2).broadcast_to([P, SLOTS * HS // 2, 2]),
+                in1=signs[:, n, :].unsqueeze(1).broadcast_to([P, SLOTS * HS // 2, 2]),
+                op=ALU.mult,
+            )
+
+        codes = [keep.tile([P, PASSES, P], U32, name="xc%d" % j, align_bytes=64) for j in range(SLOTS)]
+        scales = [keep.tile([P, PASSES, P], U8, name="xs%d" % j, align_bytes=64) for j in range(SLOTS)]
+        grouped = {}
+
+        def transpose_x(j):
+            xt = bank(6 + j % 2)
+            x_words = x_sb[j][:].bitcast(F32)
+            for g in range(PASSES):
+                for u in range(2):
+                    col = (2 * g + u) * P
+                    nc.tensor.transpose(xt[:, col : col + P], x_words[:, 256 * g + u : 256 * (g + 1) : 2], ident[:])
+            grouped[j] = stage.tile([P, C], BF16, name="grouped", align_bytes=64)
+            nc.scalar.copy(
+                out=grouped[j][:].bitcast(F32).rearrange("p (g r u) -> p g r u", g=PASSES, u=2),
+                in_=xt[:].rearrange("p (g u r) -> p g r u", g=PASSES, u=2),
+            )
+
+        def quantize_x(j):
+            nc.vector.quantize_mx(
+                out=codes[j][:].rearrange("p g r -> p (g r)").bitcast(E5M2X4),
+                scales=scales[j][:].rearrange("p g r -> p (g r)"),
+                in_=grouped[j][:],
+            )
+
+        rows = [keep.tile([P, CH, SLOTS * HS], F32, name="rows%d" % c) for c in range(6)]
+        turn = [0]
+
+        def next_bank(ring):
+            turn[0] += 1
+            return bank(turn[0] % ring)
+
+        def project(c, j, ring):
+            acc = next_bank(ring)
+            for g in range(PASSES):
+                nc.tensor.matmul_mx(
+                    out=acc[:],
+                    lhsT=codes[j][:, g, :].bitcast(E5M2X4),
+                    lhsT_scale=scales[j][:, g, :],
+                    rhs=words[c][:, g, :].bitcast(E2M1X4),
+                    rhs_scale=w_scale(c, g),
+                    start=(g == 0),
+                    stop=(g == PASSES - 1),
+                )
+            return acc
+
+        def rope_products(acc, j, cos_part, sin_part):
+            half = slice((j % 2) * HS, (j % 2 + 1) * HS)
+            freq = slice(j * HS // 2, (j + 1) * HS // 2)
+            shape = [P, CH, HS // 2, 2]
+            pairs = acc[:].rearrange("p (h i e) -> p h i e", h=CH, e=2)
+            nc.vector.tensor_tensor(
+                out=cos_part[:, :, half].rearrange("p h (i e) -> p h i e", e=2),
+                in0=pairs,
+                in1=cos_tab[:, freq, :].unsqueeze(1).broadcast_to(shape),
+                op=ALU.mult,
+            )
+            nc.vector.tensor_tensor(
+                out=sin_part[:, :, half].rearrange("p h (i e) -> p h i e", e=2),
+                in0=pairs[:, :, :, ::-1],
+                in1=sin_tab[:, freq, :].unsqueeze(1).broadcast_to(shape),
+                op=ALU.mult,
+            )
+
+        def copy_v(acc, c, j):
+            nc.scalar.copy(out=rows[c][:, :, j * HS : (j + 1) * HS], in_=acc[:].rearrange("p (h d) -> p h d", h=CH))
+
+        def store_rows(c, j_lo, j_hi):
+            for h in range(CH):
+                for b in range(B):
+                    dst = outs[c // 2][b, (c % 2) * CH + h, :, 0:TG, :].rearrange("g (q j) d -> g q (j d)", j=SLOTS)
+                    nc.sync.dma_start(
+                        out=dst[:, :, j_lo * HS : j_hi * HS], in_=rows[c][b:P:B, h, j_lo * HS : j_hi * HS]
+                    )
+
+        def add_transposed(sums, c, h, u, start, stop):
+            nc.tensor.matmul(
+                out=sums[:, (h % 4) * P : (h % 4 + 1) * P],
+                lhsT=rows[c][:, h, u * P : (u + 1) * P],
+                rhs=ident[:],
+                start=start,
+                stop=stop,
+                is_transpose=True,
+            )
+
+        group_sums = [keep.tile([P, B, CH * G], F32, name="gs%d" % c) for c in range(6)]
+
+        def slot_sums(c, half):
+            sums = bank(6 + half)
+            for h in range(4 * half, 4 * half + 4):
+                for u in range(PAIRS):
+                    add_transposed(sums, c, h, u, u == 0, u == PAIRS - 1)
+            return sums
+
+        def reduce_quarters(sums, c, half):
+            nc.vector.tensor_reduce(
+                out=group_sums[c][:, :, half * 4 * G : (half + 1) * 4 * G],
+                in_=sums[:].rearrange("p (n q b) -> p b n q", q=QUARTERS, b=B),
+                axis=mybir.AxisListType.X,
+                op=ALU.add,
+            )
+
+        def finish_means(c, ring):
+            acc = next_bank(ring)
+            for b in range(B):
+                nc.tensor.matmul(
+                    out=acc[:, b * HS : (b + 1) * HS], lhsT=group_sums[c][:, b, :], rhs=fold[:], start=True, stop=True
+                )
+            means = stage.tile([P, B, HS], F32, name="means")
+            nc.scalar.activation(
+                out=means[:], in_=acc[:, 0 : B * HS].rearrange("p (b d) -> p b d", b=B), func=ACT.Copy, scale=1.0 / TG
+            )
+            lo = (c % 2) * CH
+            dst = outs[c // 2][:, lo : lo + CH, :, TG, :].rearrange("b h g d -> (h g) b d")
+            nc.scalar.dma_start(out=dst, in_=means[:])
+
+        v_in_phase = {0: V0, 1: V1}
+        sums_in_step = {
+            5: (K1, 0), 6: (K1, 1),
+            8: (V0, 0), 9: (V0, 1), 10: (Q0, 0), 11: (Q0, 1),
+            12: (V1, 0), 13: (V1, 1), 14: (Q1, 0), 15: (Q1, 1),
+        }
+        last = ROPE_ORDER[-1]
+        last_sums = []
+        pending = None
+        finished = None
+
+        def add_last_pair(u):
+            for h in range(CH):
+                add_transposed(
+                    last_sums[h // 4], last, h, u, u == 0 and h % 4 == 0, u == PAIRS - 1 and h % 4 == 3
+                )
+
+        transpose_x(0)
+        transpose_x(1)
+        quantize_x(0)
+        quantize_x(1)
+        for step in range(4 * PAIRS):
+            phase, u = divmod(step, PAIRS)
+            c = ROPE_ORDER[phase]
+            ring = 4 if phase == 3 else 6
+            js = (2 * u, 2 * u + 1)
+            accs = [project(c, j, ring) for j in js]
+            if phase in v_in_phase:
+                for j in js:
+                    copy_v(project(v_in_phase[phase], j, ring), v_in_phase[phase], j)
+            if finished is not None:
+                finish_means(finished, ring)
+                finished = None
+            if phase == 0 and u + 1 < PAIRS:
+                transpose_x(2 * u + 2)
+                transpose_x(2 * u + 3)
+            cos_part = stage.tile([P, CH, 2 * HS], F32, name="cos_part")
+            sin_part = stage.tile([P, CH, 2 * HS], F32, name="sin_part")
+            rope_products(accs[0], js[0], cos_part, sin_part)
+            if pending is not None:
+                reduce_quarters(*pending)
+                if pending[2] == 1:
+                    finished = pending[1]
+                pending = None
+            if phase == 0 and u + 1 < PAIRS:
+                quantize_x(2 * u + 2)
+            rope_products(accs[1], js[1], cos_part, sin_part)
+            if phase == 0 and u + 1 < PAIRS:
+                quantize_x(2 * u + 3)
+            nc.gpsimd.tensor_tensor(
+                out=rows[c][:, :, u * P : (u + 1) * P], in0=cos_part[:], in1=sin_part[:], op=ALU.add
+            )
+            if step in sums_in_step:
+                pending = (slot_sums(*sums_in_step[step]),) + sums_in_step[step]
+            if phase == 3 and u >= 1:
+                if u == 1:
+                    last_sums.extend((bank(4), bank(5)))
+                add_last_pair(u - 1)
+            if u == PAIRS - 1:
+                if phase in v_in_phase:
+                    store_rows(v_in_phase[phase], 0, SLOTS)
+                if phase < 3:
+                    store_rows(c, 0, SLOTS)
+            if phase == 3 and u % 2 == 1:
+                store_rows(c, 2 * u - 2, 2 * u + 2)
+
+        reduce_quarters(*pending)
+        add_last_pair(PAIRS - 1)
+        finish_means(pending[1], 4)
+        for half in range(2):
+            reduce_quarters(last_sums[half], last, half)
+        finish_means(last, 4)

@@ -74,6 +74,11 @@ def tile_causalselfattention2_pa_kernel(
             nc.vector.memset(plane[:].bitcast(I32), 0)
 
         load_x(0)
+        cos_sb = keep.tile([P, SLOTS * HS // 2], BF16)
+        sin_sb = keep.tile([P, SLOTS * HS // 2], BF16)
+        for dst, src in ((cos_sb, freqs_cos), (sin_sb, freqs_sin)):
+            by_part = src.rearrange("(m j) i -> m (j i)", j=SLOTS)
+            nc.scalar.dma_start(out=dst[:], in_=by_part.unsqueeze(1).broadcast_to([P // B, B, SLOTS * HS // 2]))
         load_x(1)
         load_scales(0)
         load_words(K1)
@@ -87,20 +92,15 @@ def tile_causalselfattention2_pa_kernel(
 
         ident = keep.tile([P, P], F32)
         make_identity(nc, ident[:])
-        cos_sb = keep.tile([P, SLOTS * HS // 2], BF16)
-        sin_sb = keep.tile([P, SLOTS * HS // 2], BF16)
-        for dst, src in ((cos_sb, freqs_cos), (sin_sb, freqs_sin)):
-            rows = src.rearrange("(m j) i -> m (j i)", j=SLOTS)
-            nc.gpsimd.dma_start(out=dst[:], in_=rows.unsqueeze(1).broadcast_to([P // B, B, SLOTS * HS // 2]))
         fold = keep.tile([P, HS], F32)
         nc.gpsimd.tensor_tensor(out=fold[:], in0=ident[:, 0:HS], in1=ident[:, HS:P], op=ALU.add)
         signs = keep.tile([P, 2, 2], F32)
-        nc.gpsimd.memset(signs[:], 1.0)
-        nc.gpsimd.memset(signs[:, 1, 0:1], -1.0)
+        nc.vector.memset(signs[:], 1.0)
+        nc.vector.memset(signs[:, 1, 0:1], -1.0)
         cos_tab = keep.tile([P, SLOTS * HS // 2, 2], F32)
         sin_tab = keep.tile([P, SLOTS * HS // 2, 2], F32)
         for n, (tab, src) in enumerate(((cos_tab, cos_sb), (sin_tab, sin_sb))):
-            nc.gpsimd.tensor_tensor(
+            nc.vector.tensor_tensor(
                 out=tab[:],
                 in0=src[:].unsqueeze(2).broadcast_to([P, SLOTS * HS // 2, 2]),
                 in1=signs[:, n, :].unsqueeze(1).broadcast_to([P, SLOTS * HS // 2, 2]),
@@ -159,14 +159,14 @@ def tile_causalselfattention2_pa_kernel(
             pairs = acc[:].rearrange("p (h i e) -> p h i e", h=CH, e=2)
             nc.vector.tensor_tensor(
                 out=cos_part[:, :, half].rearrange("p h (i e) -> p h i e", e=2),
-                in0=pairs,
-                in1=cos_tab[:, freq, :].unsqueeze(1).broadcast_to(shape),
+                in0=cos_tab[:, freq, :].unsqueeze(1).broadcast_to(shape),
+                in1=pairs,
                 op=ALU.mult,
             )
             nc.vector.tensor_tensor(
                 out=sin_part[:, :, half].rearrange("p h (i e) -> p h i e", e=2),
-                in0=pairs[:, :, :, ::-1],
-                in1=sin_tab[:, freq, :].unsqueeze(1).broadcast_to(shape),
+                in0=sin_tab[:, freq, :].unsqueeze(1).broadcast_to(shape),
+                in1=pairs[:, :, :, ::-1],
                 op=ALU.mult,
             )
 
@@ -208,30 +208,29 @@ def tile_causalselfattention2_pa_kernel(
                 op=ALU.add,
             )
 
+        waiting_means = []
+
         def finish_means(c, ring):
             acc = next_bank(ring)
             for b in range(B):
                 nc.tensor.matmul(
                     out=acc[:, b * HS : (b + 1) * HS], lhsT=group_sums[c][:, b, :], rhs=fold[:], start=True, stop=True
                 )
-            means = stage.tile([P, B, HS], F32, name="means")
+            means = keep.tile([P, B, HS], F32, name="means%d" % c)
             nc.scalar.activation(
                 out=means[:], in_=acc[:, 0 : B * HS].rearrange("p (b d) -> p b d", b=B), func=ACT.Copy, scale=1.0 / TG
             )
-            lo = (c % 2) * CH
-            dst = outs[c // 2][:, lo : lo + CH, :, TG, :].rearrange("b h g d -> (h g) b d")
-            nc.scalar.dma_start(out=dst, in_=means[:])
+            waiting_means.append((c, means))
 
-        v_in_phase = {0: V0, 1: V1}
-        sums_in_step = {
-            5: (K1, 0), 6: (K1, 1),
-            8: (V0, 0), 9: (V0, 1), 10: (Q0, 0), 11: (Q0, 1),
-            12: (V1, 0), 13: (V1, 1), 14: (Q1, 0), 15: (Q1, 1),
-        }
+        def store_means():
+            for c, means in waiting_means:
+                lo = (c % 2) * CH
+                dst = outs[c // 2][:, lo : lo + CH, :, TG, :].rearrange("b h g d -> (h g) b d")
+                nc.sync.dma_start(out=dst, in_=means[:])
+            waiting_means.clear()
+
         last = ROPE_ORDER[-1]
         last_sums = []
-        pending = None
-        finished = None
 
         def add_last_pair(u):
             for h in range(CH):
@@ -239,58 +238,78 @@ def tile_causalselfattention2_pa_kernel(
                     last_sums[h // 4], last, h, u, u == 0 and h % 4 == 0, u == PAIRS - 1 and h % 4 == 3
                 )
 
+        def rope_add(engine, c, cos_part, sin_part, j_lo, j_hi):
+            part = slice((j_lo % 2) * HS, ((j_hi - 1) % 2 + 1) * HS)
+            engine.tensor_tensor(
+                out=rows[c][:, :, j_lo * HS : j_hi * HS], in0=cos_part[:, :, part], in1=sin_part[:, :, part], op=ALU.add
+            )
+
+        steps = len(ROPE_ORDER) * SLOTS
+        v_units = {j: [(V0, j)] for j in range(SLOTS)}
+        for j in range(SLOTS):
+            v_units[SLOTS + 2 * j] = [(V1, j)]
+        sums_in_step = {
+            9: (V0, 0), 12: (V0, 1), 15: (K1, 0), 18: (K1, 1), 21: (Q0, 0), 23: (Q0, 1), 25: (V1, 0), 27: (V1, 1),
+            29: (Q1, 0), 31: (Q1, 1),
+        }
+        to_reduce = {}
+        to_finish = {}
+
         transpose_x(0)
         transpose_x(1)
         quantize_x(0)
         quantize_x(1)
-        for step in range(4 * PAIRS):
-            phase, u = divmod(step, PAIRS)
+        for step in range(steps):
+            phase, j = divmod(step, SLOTS)
             c = ROPE_ORDER[phase]
             ring = 4 if phase == 3 else 6
-            js = (2 * u, 2 * u + 1)
-            accs = [project(c, j, ring) for j in js]
-            if phase in v_in_phase:
-                for j in js:
-                    copy_v(project(v_in_phase[phase], j, ring), v_in_phase[phase], j)
-            if finished is not None:
-                finish_means(finished, ring)
-                finished = None
-            if phase == 0 and u + 1 < PAIRS:
-                transpose_x(2 * u + 2)
-                transpose_x(2 * u + 3)
-            cos_part = stage.tile([P, CH, 2 * HS], F32, name="cos_part")
-            sin_part = stage.tile([P, CH, 2 * HS], F32, name="sin_part")
-            rope_products(accs[0], js[0], cos_part, sin_part)
-            if pending is not None:
-                reduce_quarters(*pending)
-                if pending[2] == 1:
-                    finished = pending[1]
-                pending = None
-            if phase == 0 and u + 1 < PAIRS:
-                quantize_x(2 * u + 2)
-            rope_products(accs[1], js[1], cos_part, sin_part)
-            if phase == 0 and u + 1 < PAIRS:
-                quantize_x(2 * u + 3)
-            nc.gpsimd.tensor_tensor(
-                out=rows[c][:, :, u * P : (u + 1) * P], in0=cos_part[:], in1=sin_part[:], op=ALU.add
-            )
+            acc = project(c, j, ring)
+            for vc, vj in v_units.get(step, ()):
+                copy_v(project(vc, vj, ring), vc, vj)
+            if step in to_finish:
+                finish_means(to_finish[step], ring)
+            if 2 * step + 2 < SLOTS:
+                transpose_x(2 * step + 2)
+                transpose_x(2 * step + 3)
+            if j % 2 == 0:
+                cos_part = stage.tile([P, CH, 2 * HS], F32, name="cos_part")
+                sin_part = stage.tile([P, CH, 2 * HS], F32, name="sin_part")
+            rope_products(acc, j, cos_part, sin_part)
+            if 2 * step + 2 < SLOTS:
+                quantize_x(2 * step + 2)
+                quantize_x(2 * step + 3)
+            if step in to_reduce:
+                reduce_quarters(*to_reduce[step])
+            if step < 4:
+                rope_add(nc.vector if step < 3 else nc.gpsimd, c, cos_part, sin_part, j, j + 1)
+            elif j % 2 == 1:
+                rope_add(nc.gpsimd if step < steps - 1 else nc.vector, c, cos_part, sin_part, j - 1, j + 1)
             if step in sums_in_step:
-                pending = (slot_sums(*sums_in_step[step]),) + sums_in_step[step]
-            if phase == 3 and u >= 1:
-                if u == 1:
+                sc, half = sums_in_step[step]
+                to_reduce[step + 1] = (slot_sums(sc, half), sc, half)
+                if half == 1:
+                    to_finish[step + 4] = sc
+            if phase == 3 and j in (4, 6):
+                if j == 4:
                     last_sums.extend((bank(4), bank(5)))
-                add_last_pair(u - 1)
-            if u == PAIRS - 1:
-                if phase in v_in_phase:
-                    store_rows(v_in_phase[phase], 0, SLOTS)
+                add_last_pair(j // 2 - 2)
+            if j == SLOTS - 1:
+                store_means()
+                if phase == 0:
+                    store_rows(V0, 0, SLOTS)
+                if phase == 2:
+                    store_rows(V1, 0, SLOTS)
                 if phase < 3:
                     store_rows(c, 0, SLOTS)
-            if phase == 3 and u % 2 == 1:
-                store_rows(c, 2 * u - 2, 2 * u + 2)
+            if phase == 3 and j == 3:
+                store_rows(c, 0, SLOTS // 2)
 
-        reduce_quarters(*pending)
+        store_rows(last, SLOTS // 2, SLOTS)
+        add_last_pair(PAIRS - 2)
+        reduce_quarters(*to_reduce[steps])
         add_last_pair(PAIRS - 1)
-        finish_means(pending[1], 4)
+        finish_means(Q1, 4)
         for half in range(2):
             reduce_quarters(last_sums[half], last, half)
         finish_means(last, 4)
+        store_means()

@@ -6,6 +6,7 @@ from concourse.masks import make_identity
 B, T, C, H, G = 2, 512, 1024, 16, 16
 HS = C // H
 TG = T // G
+FREQS = HS // 2
 FLOPS = 2 * B * T * C * 3 * C
 
 F32 = mybir.dt.float32
@@ -17,16 +18,33 @@ E5M2X4 = mybir.dt.float8_e5m2_x4
 E2M1X4 = mybir.dt.float4_e2m1fn_x4
 ALU = mybir.AluOpType
 ACT = mybir.ActivationFunctionType
+AXIS_X = mybir.AxisListType.X
 
 P = 128
 SLOTS = B * T // P
 PAIRS = SLOTS // 2
 QUARTERS = TG // SLOTS
-PASSES = C // 512
+K_PASS = 4 * P
+PASSES = C // K_PASS
 NCOL = 512
 CH = NCOL // HS
-Q0, Q1, K0, K1, V0, V1 = range(6)
+HALF = CH // 2
+CHUNKS = 3 * C // NCOL
+Q0, Q1, K0, K1, V0, V1 = range(CHUNKS)
+
 ROPE_ORDER = (K1, Q0, Q1, K0)
+STEPS = len(ROPE_ORDER) * SLOTS
+LAST = ROPE_ORDER[-1]
+
+RING, LAST_RING = 6, 4
+SUM_BANK, LAST_SUM_BANK = 6, 4
+
+V1_EVERY = 2
+SUMS_FIRST, SUMS_EVERY = 10, 3
+SUM_ORDER = (V0, K1, Q0, Q1)
+FOLD_AFTER = 4
+VECTOR_ADDS = 3
+PART_BUFS = 4
 
 
 def tile_causalselfattention2_pa_kernel(
@@ -46,8 +64,8 @@ def tile_causalselfattention2_pa_kernel(
 
         x_sb = [keep.tile([P, C], BF16, name="x%d" % j) for j in range(SLOTS)]
         x_view = x.rearrange("b (m j) c -> m b j c", j=SLOTS)
-        words = [keep.tile([P, PASSES, 2 * NCOL], U8, name="w%d" % c, align_bytes=64) for c in range(6)]
-        spans = ((K1, V1), (Q0, K1), (V1, V1 + 1))
+        words = [keep.tile([P, PASSES, 2 * NCOL], U8, name="w%d" % c, align_bytes=64) for c in range(CHUNKS)]
+        spans = ((K1, V1), (Q0, K1), (V1, CHUNKS))
         planes = [
             keep.tile([P, PASSES, (hi - lo) * NCOL], U8, name="plane%d" % lo, align_bytes=64) for lo, hi in spans
         ]
@@ -67,18 +85,18 @@ def tile_causalselfattention2_pa_kernel(
         def load_scales(n):
             lo, hi = spans[n]
             for quad in range(4):
-                src = w_attn_scales[:, 4 * quad : 4 * quad + 4, lo * NCOL : hi * NCOL].rearrange("g r n -> r g n")
+                src = w_attn_scales[:, 4 * quad : 4 * quad + 4, lo * NCOL : hi * NCOL].rearrange("g i n -> i g n")
                 nc.sync.dma_start(out=planes[n][32 * quad : 32 * quad + 4, :, :].bitcast(I32), in_=src.bitcast(I32))
 
         for plane in planes:
             nc.vector.memset(plane[:].bitcast(I32), 0)
 
         load_x(0)
-        cos_sb = keep.tile([P, SLOTS * HS // 2], BF16)
-        sin_sb = keep.tile([P, SLOTS * HS // 2], BF16)
+        cos_sb = keep.tile([P, SLOTS * FREQS], BF16)
+        sin_sb = keep.tile([P, SLOTS * FREQS], BF16)
         for dst, src in ((cos_sb, freqs_cos), (sin_sb, freqs_sin)):
             by_part = src.rearrange("(m j) i -> m (j i)", j=SLOTS)
-            nc.scalar.dma_start(out=dst[:], in_=by_part.unsqueeze(1).broadcast_to([P // B, B, SLOTS * HS // 2]))
+            nc.scalar.dma_start(out=dst[:], in_=by_part.unsqueeze(1).broadcast_to([P // B, B, SLOTS * FREQS]))
         load_x(1)
         load_scales(0)
         load_words(K1)
@@ -92,18 +110,26 @@ def tile_causalselfattention2_pa_kernel(
 
         ident = keep.tile([P, P], F32)
         make_identity(nc, ident[:])
+        group_of = keep.tile([P, P], F32)
+        nc.vector.memset(group_of[:], 0.0)
+        nc.vector.tensor_reduce(
+            out=group_of[:, 0:P:QUARTERS].rearrange("p (b g) -> p b g", b=B),
+            in_=ident[:].rearrange("p (g r b) -> p b g r", r=QUARTERS, b=B),
+            axis=AXIS_X,
+            op=ALU.add,
+        )
         fold = keep.tile([P, HS], F32)
         nc.gpsimd.tensor_tensor(out=fold[:], in0=ident[:, 0:HS], in1=ident[:, HS:P], op=ALU.add)
         signs = keep.tile([P, 2, 2], F32)
         nc.vector.memset(signs[:], 1.0)
         nc.vector.memset(signs[:, 1, 0:1], -1.0)
-        cos_tab = keep.tile([P, SLOTS * HS // 2, 2], F32)
-        sin_tab = keep.tile([P, SLOTS * HS // 2, 2], F32)
+        cos_tab = keep.tile([P, SLOTS * FREQS, 2], F32)
+        sin_tab = keep.tile([P, SLOTS * FREQS, 2], F32)
         for n, (tab, src) in enumerate(((cos_tab, cos_sb), (sin_tab, sin_sb))):
             nc.vector.tensor_tensor(
                 out=tab[:],
-                in0=src[:].unsqueeze(2).broadcast_to([P, SLOTS * HS // 2, 2]),
-                in1=signs[:, n, :].unsqueeze(1).broadcast_to([P, SLOTS * HS // 2, 2]),
+                in0=src[:].unsqueeze(2).broadcast_to([P, SLOTS * FREQS, 2]),
+                in1=signs[:, n, :].unsqueeze(1).broadcast_to([P, SLOTS * FREQS, 2]),
                 op=ALU.mult,
             )
 
@@ -111,32 +137,35 @@ def tile_causalselfattention2_pa_kernel(
         scales = [keep.tile([P, PASSES, P], U8, name="xs%d" % j, align_bytes=64) for j in range(SLOTS)]
         grouped = {}
 
-        def transpose_x(j):
-            xt = bank(6 + j % 2)
+        def transpose_x(j, passes, bank_no):
+            if passes.start == 0:
+                grouped[j] = stage.tile([P, C], BF16, name="grouped", align_bytes=64)
+            xt = bank(bank_no)
             x_words = x_sb[j][:].bitcast(F32)
-            for g in range(PASSES):
+            for g in passes:
                 for u in range(2):
-                    col = (2 * g + u) * P
+                    col = (2 * (g - passes.start) + u) * P
                     nc.tensor.transpose(xt[:, col : col + P], x_words[:, 256 * g + u : 256 * (g + 1) : 2], ident[:])
-            grouped[j] = stage.tile([P, C], BF16, name="grouped", align_bytes=64)
             nc.scalar.copy(
-                out=grouped[j][:].bitcast(F32).rearrange("p (g r u) -> p g r u", g=PASSES, u=2),
-                in_=xt[:].rearrange("p (g u r) -> p g r u", g=PASSES, u=2),
+                out=grouped[j][:, passes.start * K_PASS : passes.stop * K_PASS]
+                .bitcast(F32)
+                .rearrange("p (g n u) -> p g n u", g=len(passes), u=2),
+                in_=xt[:, 0 : len(passes) * 2 * P].rearrange("p (g u n) -> p g n u", g=len(passes), u=2),
             )
 
-        def quantize_x(j):
+        def quantize_x(j, passes):
             nc.vector.quantize_mx(
-                out=codes[j][:].rearrange("p g r -> p (g r)").bitcast(E5M2X4),
-                scales=scales[j][:].rearrange("p g r -> p (g r)"),
-                in_=grouped[j][:],
+                out=codes[j][:, passes.start : passes.stop, :].rearrange("p g n -> p (g n)").bitcast(E5M2X4),
+                scales=scales[j][:, passes.start : passes.stop, :].rearrange("p g n -> p (g n)"),
+                in_=grouped[j][:, passes.start * K_PASS : passes.stop * K_PASS],
             )
 
-        rows = [keep.tile([P, CH, SLOTS * HS], F32, name="rows%d" % c) for c in range(6)]
-        turn = [0]
+        rows = [keep.tile([P, CH, SLOTS * HS], F32, name="rows%d" % c) for c in range(CHUNKS)]
+        taken = []
 
         def next_bank(ring):
-            turn[0] += 1
-            return bank(turn[0] % ring)
+            taken.append(ring)
+            return bank(len(taken) % ring)
 
         def project(c, j, ring):
             acc = next_bank(ring)
@@ -152,38 +181,55 @@ def tile_causalselfattention2_pa_kernel(
                 )
             return acc
 
-        def rope_products(acc, j, cos_part, sin_part):
-            half = slice((j % 2) * HS, (j % 2 + 1) * HS)
-            freq = slice(j * HS // 2, (j + 1) * HS // 2)
-            shape = [P, CH, HS // 2, 2]
-            pairs = acc[:].rearrange("p (h i e) -> p h i e", h=CH, e=2)
+        def rope_products(acc, j, cos_part, sin_part, heads):
+            place = slice((j % 2) * HS, (j % 2 + 1) * HS)
+            freq = slice(j * FREQS, (j + 1) * FREQS)
+            shape = [P, heads.stop - heads.start, FREQS, 2]
+            pairs = acc[:].rearrange("p (h i e) -> p h i e", h=CH, e=2)[:, heads]
             nc.vector.tensor_tensor(
-                out=cos_part[:, :, half].rearrange("p h (i e) -> p h i e", e=2),
+                out=cos_part[:, heads, place].rearrange("p h (i e) -> p h i e", e=2),
                 in0=cos_tab[:, freq, :].unsqueeze(1).broadcast_to(shape),
                 in1=pairs,
                 op=ALU.mult,
             )
             nc.vector.tensor_tensor(
-                out=sin_part[:, :, half].rearrange("p h (i e) -> p h i e", e=2),
+                out=sin_part[:, heads, place].rearrange("p h (i e) -> p h i e", e=2),
                 in0=sin_tab[:, freq, :].unsqueeze(1).broadcast_to(shape),
                 in1=pairs[:, :, :, ::-1],
                 op=ALU.mult,
             )
 
-        def copy_v(acc, c, j):
-            nc.scalar.copy(out=rows[c][:, :, j * HS : (j + 1) * HS], in_=acc[:].rearrange("p (h d) -> p h d", h=CH))
+        def rope_add(engine, c, cos_part, sin_part, j_lo, j_hi, heads):
+            place = slice((j_lo % 2) * HS, ((j_hi - 1) % 2 + 1) * HS)
+            engine.tensor_tensor(
+                out=rows[c][:, heads, j_lo * HS : j_hi * HS],
+                in0=cos_part[:, heads, place],
+                in1=sin_part[:, heads, place],
+                op=ALU.add,
+            )
+
+        def by_head(acc):
+            return acc[:].rearrange("p (h d) -> p h d", h=CH)
+
+        def copy_v(c, j, ring):
+            acc = project(c, j, ring)
+            nc.scalar.copy(out=rows[c][:, :, j * HS : (j + 1) * HS], in_=by_head(acc))
+            return acc
 
         def store_rows(c, j_lo, j_hi):
             for h in range(CH):
                 for b in range(B):
-                    dst = outs[c // 2][b, (c % 2) * CH + h, :, 0:TG, :].rearrange("g (q j) d -> g q (j d)", j=SLOTS)
+                    dst = outs[c // 2][b, (c % 2) * CH + h, :, 0:TG, :].rearrange("g (r j) d -> g r (j d)", j=SLOTS)
                     nc.sync.dma_start(
                         out=dst[:, :, j_lo * HS : j_hi * HS], in_=rows[c][b:P:B, h, j_lo * HS : j_hi * HS]
                     )
 
+        group_sums = {c: keep.tile([P, B, CH * G], F32, name="gs%d" % c) for c in SUM_ORDER + (LAST,)}
+        waiting_means = []
+
         def add_transposed(sums, c, h, u, start, stop):
             nc.tensor.matmul(
-                out=sums[:, (h % 4) * P : (h % 4 + 1) * P],
+                out=sums[:, (h % HALF) * P : (h % HALF + 1) * P],
                 lhsT=rows[c][:, h, u * P : (u + 1) * P],
                 rhs=ident[:],
                 start=start,
@@ -191,26 +237,40 @@ def tile_causalselfattention2_pa_kernel(
                 is_transpose=True,
             )
 
-        group_sums = [keep.tile([P, B, CH * G], F32, name="gs%d" % c) for c in range(6)]
-
         def slot_sums(c, half):
-            sums = bank(6 + half)
-            for h in range(4 * half, 4 * half + 4):
+            sums = bank(SUM_BANK + half)
+            for h in range(HALF * half, HALF * (half + 1)):
                 for u in range(PAIRS):
                     add_transposed(sums, c, h, u, u == 0, u == PAIRS - 1)
             return sums
 
+        last_sums = []
+
+        def add_last_pair(u):
+            if u == 0:
+                last_sums.extend((bank(LAST_SUM_BANK), bank(LAST_SUM_BANK + 1)))
+            for h in range(CH):
+                first = u == 0 and h % HALF == 0
+                final = u == PAIRS - 1 and h % HALF == HALF - 1
+                add_transposed(last_sums[h // HALF], LAST, h, u, first, final)
+
         def reduce_quarters(sums, c, half):
-            nc.vector.tensor_reduce(
-                out=group_sums[c][:, :, half * 4 * G : (half + 1) * 4 * G],
-                in_=sums[:].rearrange("p (n q b) -> p b n q", q=QUARTERS, b=B),
-                axis=mybir.AxisListType.X,
-                op=ALU.add,
-            )
+            dst = group_sums[c][:, :, half * HALF * G : (half + 1) * HALF * G]
+            if c == V0:
+                by_quarter = stage.tile([P, QUARTERS, B, HALF * G], F32, name="by_quarter")
+                nc.scalar.copy(out=by_quarter[:], in_=sums[:].rearrange("p (n r b) -> p r b n", r=QUARTERS, b=B))
+                halved = stage.tile([P, 2, B, HALF * G], F32, name="halved")
+                nc.gpsimd.tensor_tensor(out=halved[:], in0=by_quarter[:, 0:2], in1=by_quarter[:, 2:4], op=ALU.add)
+                nc.gpsimd.tensor_tensor(out=dst, in0=halved[:, 0], in1=halved[:, 1], op=ALU.add)
+            else:
+                nc.vector.tensor_reduce(
+                    out=dst, in_=sums[:].rearrange("p (n r b) -> p b n r", r=QUARTERS, b=B), axis=AXIS_X, op=ALU.add
+                )
 
-        waiting_means = []
+        def mean_rows(c):
+            return outs[c // 2][:, (c % 2) * CH : (c % 2 + 1) * CH, :, TG, :]
 
-        def finish_means(c, ring):
+        def fold_means(c, ring):
             acc = next_bank(ring)
             for b in range(B):
                 nc.tensor.matmul(
@@ -220,96 +280,116 @@ def tile_causalselfattention2_pa_kernel(
             nc.scalar.activation(
                 out=means[:], in_=acc[:, 0 : B * HS].rearrange("p (b d) -> p b d", b=B), func=ACT.Copy, scale=1.0 / TG
             )
-            waiting_means.append((c, means))
+            waiting_means.append((mean_rows(c).rearrange("b h g d -> (h g) b d"), means[:]))
+
+        v1_sum = keep.tile([P, CH, HS], F32)
+
+        def add_v1_slot(acc, j):
+            so_far = rows[V1][:, :, 0:HS] if j == 1 else v1_sum[:]
+            nc.vector.tensor_tensor(out=v1_sum[:], in0=so_far, in1=by_head(acc), op=ALU.add)
+
+        def v1_means(ring):
+            acc = next_bank(ring)
+            nc.tensor.matmul(
+                out=acc[:], lhsT=group_of[:], rhs=v1_sum[:].rearrange("p h d -> p (h d)"), start=True, stop=True
+            )
+            means = keep.tile([P, CH, HS], F32, name="means%d" % V1)
+            nc.scalar.activation(out=means[:], in_=by_head(acc), func=ACT.Copy, scale=1.0 / TG)
+            for b in range(B):
+                src = means[b * P // B : (b + 1) * P // B : QUARTERS, :, :]
+                waiting_means.append((mean_rows(V1)[b].rearrange("h g d -> g h d"), src))
 
         def store_means():
-            for c, means in waiting_means:
-                lo = (c % 2) * CH
-                dst = outs[c // 2][:, lo : lo + CH, :, TG, :].rearrange("b h g d -> (h g) b d")
-                nc.sync.dma_start(out=dst, in_=means[:])
+            for dst, src in waiting_means:
+                nc.sync.dma_start(out=dst, in_=src)
             waiting_means.clear()
 
-        last = ROPE_ORDER[-1]
-        last_sums = []
-
-        def add_last_pair(u):
-            for h in range(CH):
-                add_transposed(
-                    last_sums[h // 4], last, h, u, u == 0 and h % 4 == 0, u == PAIRS - 1 and h % 4 == 3
-                )
-
-        def rope_add(engine, c, cos_part, sin_part, j_lo, j_hi):
-            part = slice((j_lo % 2) * HS, ((j_hi - 1) % 2 + 1) * HS)
-            engine.tensor_tensor(
-                out=rows[c][:, :, j_lo * HS : j_hi * HS], in0=cos_part[:, :, part], in1=sin_part[:, :, part], op=ALU.add
-            )
-
-        steps = len(ROPE_ORDER) * SLOTS
-        v_units = {j: [(V0, j)] for j in range(SLOTS)}
-        for j in range(SLOTS):
-            v_units[SLOTS + 2 * j] = [(V1, j)]
+        all_passes = range(PASSES)
+        all_heads = slice(0, CH)
+        halves = [slice(HALF * half, HALF * (half + 1)) for half in range(2)]
         sums_in_step = {
-            9: (V0, 0), 12: (V0, 1), 15: (K1, 0), 18: (K1, 1), 21: (Q0, 0), 23: (Q0, 1), 25: (V1, 0), 27: (V1, 1),
-            29: (Q1, 0), 31: (Q1, 1),
+            SUMS_FIRST + SUMS_EVERY * n: (SUM_ORDER[n // 2], n % 2) for n in range(2 * len(SUM_ORDER))
         }
+        v1_done = SLOTS + V1_EVERY * (SLOTS - 1)
         to_reduce = {}
-        to_finish = {}
+        to_fold = {}
 
-        transpose_x(0)
-        transpose_x(1)
-        quantize_x(0)
-        quantize_x(1)
-        for step in range(steps):
+        for g in all_passes:
+            transpose_x(0, range(g, g + 1), SUM_BANK + g)
+            quantize_x(0, range(g, g + 1))
+        transpose_x(1, all_passes, RING - 1)
+        quantize_x(1, all_passes)
+
+        for step in range(STEPS):
             phase, j = divmod(step, SLOTS)
             c = ROPE_ORDER[phase]
-            ring = 4 if phase == 3 else 6
+            ring = LAST_RING if c == LAST else RING
+            new_slots = [n for n in (2 * step + 2, 2 * step + 3) if n < SLOTS]
+            v1_slot, off_beat = divmod(step - SLOTS, V1_EVERY)
+            v1_now = off_beat == 0 and 0 <= v1_slot < SLOTS
+
             acc = project(c, j, ring)
-            for vc, vj in v_units.get(step, ()):
-                copy_v(project(vc, vj, ring), vc, vj)
-            if step in to_finish:
-                finish_means(to_finish[step], ring)
-            if 2 * step + 2 < SLOTS:
-                transpose_x(2 * step + 2)
-                transpose_x(2 * step + 3)
+            if phase == 0:
+                copy_v(V0, j, ring)
+            if v1_now:
+                v1_acc = copy_v(V1, v1_slot, ring)
+            if step == v1_done + FOLD_AFTER:
+                v1_means(ring)
+            if step in to_fold:
+                fold_means(to_fold[step], ring)
+            for n in new_slots:
+                transpose_x(n, all_passes, SUM_BANK + n % 2)
             if j % 2 == 0:
-                cos_part = stage.tile([P, CH, 2 * HS], F32, name="cos_part")
-                sin_part = stage.tile([P, CH, 2 * HS], F32, name="sin_part")
-            rope_products(acc, j, cos_part, sin_part)
-            if 2 * step + 2 < SLOTS:
-                quantize_x(2 * step + 2)
-                quantize_x(2 * step + 3)
+                cos_part = stage.tile([P, CH, 2 * HS], F32, name="cos_part", bufs=PART_BUFS)
+                sin_part = stage.tile([P, CH, 2 * HS], F32, name="sin_part", bufs=PART_BUFS)
+            if step == STEPS - 1:
+                break
+
+            rope_products(acc, j, cos_part, sin_part, all_heads)
+            for n in new_slots:
+                quantize_x(n, all_passes)
+            if v1_now and v1_slot > 0:
+                add_v1_slot(v1_acc, v1_slot)
             if step in to_reduce:
                 reduce_quarters(*to_reduce[step])
-            if step < 4:
-                rope_add(nc.vector if step < 3 else nc.gpsimd, c, cos_part, sin_part, j, j + 1)
+            if step < VECTOR_ADDS:
+                rope_add(nc.vector, c, cos_part, sin_part, j, j + 1, all_heads)
+            elif step in (VECTOR_ADDS, STEPS - 2):
+                rope_add(nc.gpsimd, c, cos_part, sin_part, j, j + 1, all_heads)
             elif j % 2 == 1:
-                rope_add(nc.gpsimd if step < steps - 1 else nc.vector, c, cos_part, sin_part, j - 1, j + 1)
+                rope_add(nc.gpsimd, c, cos_part, sin_part, j - 1, j + 1, all_heads)
+
             if step in sums_in_step:
-                sc, half = sums_in_step[step]
-                to_reduce[step + 1] = (slot_sums(sc, half), sc, half)
+                sum_chunk, half = sums_in_step[step]
+                to_reduce[step + 1] = (slot_sums(sum_chunk, half), sum_chunk, half)
                 if half == 1:
-                    to_finish[step + 4] = sc
-            if phase == 3 and j in (4, 6):
-                if j == 4:
-                    last_sums.extend((bank(4), bank(5)))
-                add_last_pair(j // 2 - 2)
+                    to_fold[step + FOLD_AFTER] = sum_chunk
+            if step in (STEPS - 3, STEPS - 2):
+                add_last_pair(step - (STEPS - 3))
+
+            if step == v1_done:
+                store_rows(V1, 0, SLOTS)
             if j == SLOTS - 1:
                 store_means()
                 if phase == 0:
                     store_rows(V0, 0, SLOTS)
-                if phase == 2:
-                    store_rows(V1, 0, SLOTS)
-                if phase < 3:
-                    store_rows(c, 0, SLOTS)
-            if phase == 3 and j == 3:
+                store_rows(c, 0, SLOTS)
+            if c == LAST and j == SLOTS // 2 - 1:
                 store_rows(c, 0, SLOTS // 2)
 
-        store_rows(last, SLOTS // 2, SLOTS)
+        sum_chunk, half = sums_in_step[STEPS - 1]
+        sums = slot_sums(sum_chunk, half)
         add_last_pair(PAIRS - 2)
-        reduce_quarters(*to_reduce[steps])
+        for heads in halves:
+            rope_products(acc, j, cos_part, sin_part, heads)
+        for heads in halves:
+            rope_add(nc.vector, LAST, cos_part, sin_part, j, j + 1, heads)
+        store_means()
+        store_rows(LAST, SLOTS // 2, SLOTS)
+        reduce_quarters(sums, sum_chunk, half)
         add_last_pair(PAIRS - 1)
-        finish_means(Q1, 4)
+        fold_means(sum_chunk, LAST_RING)
         for half in range(2):
-            reduce_quarters(last_sums[half], last, half)
-        finish_means(last, 4)
+            reduce_quarters(last_sums[half], LAST, half)
+        fold_means(LAST, LAST_RING)
         store_means()

@@ -40,8 +40,8 @@ RING, LAST_RING = 6, 4
 SUM_BANK, LAST_SUM_BANK = 6, 4
 
 V1_EVERY = 2
-SUMS_FIRST, SUMS_EVERY = 10, 3
-SUM_ORDER = (V0, K1, Q0, Q1)
+SUM_ORDER = (V0, K1, Q0, V1, Q1)
+SUMS_BESIDE_V1, SUMS_LATER = 3, 2
 FOLD_AFTER = 4
 VECTOR_ADDS = 3
 PART_BUFS = 4
@@ -110,14 +110,6 @@ def tile_causalselfattention2_pa_kernel(
 
         ident = keep.tile([P, P], F32)
         make_identity(nc, ident[:])
-        group_of = keep.tile([P, P], F32)
-        nc.vector.memset(group_of[:], 0.0)
-        nc.vector.tensor_reduce(
-            out=group_of[:, 0:P:QUARTERS].rearrange("p (b g) -> p b g", b=B),
-            in_=ident[:].rearrange("p (g r b) -> p b g r", r=QUARTERS, b=B),
-            axis=AXIS_X,
-            op=ALU.add,
-        )
         fold = keep.tile([P, HS], F32)
         nc.gpsimd.tensor_tensor(out=fold[:], in0=ident[:, 0:HS], in1=ident[:, HS:P], op=ALU.add)
         signs = keep.tile([P, 2, 2], F32)
@@ -208,13 +200,9 @@ def tile_causalselfattention2_pa_kernel(
                 op=ALU.add,
             )
 
-        def by_head(acc):
-            return acc[:].rearrange("p (h d) -> p h d", h=CH)
-
         def copy_v(c, j, ring):
             acc = project(c, j, ring)
-            nc.scalar.copy(out=rows[c][:, :, j * HS : (j + 1) * HS], in_=by_head(acc))
-            return acc
+            nc.scalar.copy(out=rows[c][:, :, j * HS : (j + 1) * HS], in_=acc[:].rearrange("p (h d) -> p h d", h=CH))
 
         def store_rows(c, j_lo, j_hi):
             for h in range(CH):
@@ -256,19 +244,9 @@ def tile_causalselfattention2_pa_kernel(
 
         def reduce_quarters(sums, c, half):
             dst = group_sums[c][:, :, half * HALF * G : (half + 1) * HALF * G]
-            if c == V0:
-                by_quarter = stage.tile([P, QUARTERS, B, HALF * G], F32, name="by_quarter")
-                nc.scalar.copy(out=by_quarter[:], in_=sums[:].rearrange("p (n r b) -> p r b n", r=QUARTERS, b=B))
-                halved = stage.tile([P, 2, B, HALF * G], F32, name="halved")
-                nc.gpsimd.tensor_tensor(out=halved[:], in0=by_quarter[:, 0:2], in1=by_quarter[:, 2:4], op=ALU.add)
-                nc.gpsimd.tensor_tensor(out=dst, in0=halved[:, 0], in1=halved[:, 1], op=ALU.add)
-            else:
-                nc.vector.tensor_reduce(
-                    out=dst, in_=sums[:].rearrange("p (n r b) -> p b n r", r=QUARTERS, b=B), axis=AXIS_X, op=ALU.add
-                )
-
-        def mean_rows(c):
-            return outs[c // 2][:, (c % 2) * CH : (c % 2 + 1) * CH, :, TG, :]
+            nc.vector.tensor_reduce(
+                out=dst, in_=sums[:].rearrange("p (n r b) -> p b n r", r=QUARTERS, b=B), axis=AXIS_X, op=ALU.add
+            )
 
         def fold_means(c, ring):
             acc = next_bank(ring)
@@ -280,24 +258,8 @@ def tile_causalselfattention2_pa_kernel(
             nc.scalar.activation(
                 out=means[:], in_=acc[:, 0 : B * HS].rearrange("p (b d) -> p b d", b=B), func=ACT.Copy, scale=1.0 / TG
             )
-            waiting_means.append((mean_rows(c).rearrange("b h g d -> (h g) b d"), means[:]))
-
-        v1_sum = keep.tile([P, CH, HS], F32)
-
-        def add_v1_slot(acc, j):
-            so_far = rows[V1][:, :, 0:HS] if j == 1 else v1_sum[:]
-            nc.vector.tensor_tensor(out=v1_sum[:], in0=so_far, in1=by_head(acc), op=ALU.add)
-
-        def v1_means(ring):
-            acc = next_bank(ring)
-            nc.tensor.matmul(
-                out=acc[:], lhsT=group_of[:], rhs=v1_sum[:].rearrange("p h d -> p (h d)"), start=True, stop=True
-            )
-            means = keep.tile([P, CH, HS], F32, name="means%d" % V1)
-            nc.scalar.activation(out=means[:], in_=by_head(acc), func=ACT.Copy, scale=1.0 / TG)
-            for b in range(B):
-                src = means[b * P // B : (b + 1) * P // B : QUARTERS, :, :]
-                waiting_means.append((mean_rows(V1)[b].rearrange("h g d -> g h d"), src))
+            dst = outs[c // 2][:, (c % 2) * CH : (c % 2 + 1) * CH, :, TG, :].rearrange("b h g d -> (h g) b d")
+            waiting_means.append((dst, means[:]))
 
         def store_means():
             for dst, src in waiting_means:
@@ -307,9 +269,9 @@ def tile_causalselfattention2_pa_kernel(
         all_passes = range(PASSES)
         all_heads = slice(0, CH)
         halves = [slice(HALF * half, HALF * (half + 1)) for half in range(2)]
-        sums_in_step = {
-            SUMS_FIRST + SUMS_EVERY * n: (SUM_ORDER[n // 2], n % 2) for n in range(2 * len(SUM_ORDER))
-        }
+        sum_steps = [SLOTS + 1 + SUMS_BESIDE_V1 * n for n in range(2 * SUM_ORDER.index(Q0))]
+        sum_steps += [STEPS - 1 - SUMS_LATER * n for n in reversed(range(2 * len(SUM_ORDER) - len(sum_steps)))]
+        sums_in_step = {step: (SUM_ORDER[n // 2], n % 2) for n, step in enumerate(sum_steps)}
         v1_done = SLOTS + V1_EVERY * (SLOTS - 1)
         to_reduce = {}
         to_fold = {}
@@ -326,15 +288,12 @@ def tile_causalselfattention2_pa_kernel(
             ring = LAST_RING if c == LAST else RING
             new_slots = [n for n in (2 * step + 2, 2 * step + 3) if n < SLOTS]
             v1_slot, off_beat = divmod(step - SLOTS, V1_EVERY)
-            v1_now = off_beat == 0 and 0 <= v1_slot < SLOTS
 
             acc = project(c, j, ring)
             if phase == 0:
                 copy_v(V0, j, ring)
-            if v1_now:
-                v1_acc = copy_v(V1, v1_slot, ring)
-            if step == v1_done + FOLD_AFTER:
-                v1_means(ring)
+            if off_beat == 0 and 0 <= v1_slot < SLOTS:
+                copy_v(V1, v1_slot, ring)
             if step in to_fold:
                 fold_means(to_fold[step], ring)
             for n in new_slots:
@@ -348,8 +307,6 @@ def tile_causalselfattention2_pa_kernel(
             rope_products(acc, j, cos_part, sin_part, all_heads)
             for n in new_slots:
                 quantize_x(n, all_passes)
-            if v1_now and v1_slot > 0:
-                add_v1_slot(v1_acc, v1_slot)
             if step in to_reduce:
                 reduce_quarters(*to_reduce[step])
             if step < VECTOR_ADDS:
@@ -364,8 +321,8 @@ def tile_causalselfattention2_pa_kernel(
                 to_reduce[step + 1] = (slot_sums(sum_chunk, half), sum_chunk, half)
                 if half == 1:
                     to_fold[step + FOLD_AFTER] = sum_chunk
-            if step in (STEPS - 3, STEPS - 2):
-                add_last_pair(step - (STEPS - 3))
+            if c == LAST and j in (4, 6):
+                add_last_pair(j // 2 - 2)
 
             if step == v1_done:
                 store_rows(V1, 0, SLOTS)

@@ -39,9 +39,10 @@ LAST = ROPE_ORDER[-1]
 RING, LAST_RING = 6, 4
 SUM_BANK, LAST_SUM_BANK = 6, 4
 
-V1_EVERY = 2
-SUM_ORDER = (V0, K1, Q0, V1, Q1)
-SUMS_BESIDE_V1, SUMS_LATER = 3, 2
+V_BESIDE = (V0, V1)
+SUM_ORDER = (V0, K1, V1, Q0, Q1)
+SUMS_EVERY = 2
+STORED_IN_HALVES = (V0, LAST)
 FOLD_AFTER = 4
 VECTOR_ADDS = 3
 PART_BUFS = 4
@@ -269,10 +270,8 @@ def tile_causalselfattention2_pa_kernel(
         all_passes = range(PASSES)
         all_heads = slice(0, CH)
         halves = [slice(HALF * half, HALF * (half + 1)) for half in range(2)]
-        sum_steps = [SLOTS + 1 + SUMS_BESIDE_V1 * n for n in range(2 * SUM_ORDER.index(Q0))]
-        sum_steps += [STEPS - 1 - SUMS_LATER * n for n in reversed(range(2 * len(SUM_ORDER) - len(sum_steps)))]
+        sum_steps = range(STEPS - 1 - SUMS_EVERY * (2 * len(SUM_ORDER) - 1), STEPS, SUMS_EVERY)
         sums_in_step = {step: (SUM_ORDER[n // 2], n % 2) for n, step in enumerate(sum_steps)}
-        v1_done = SLOTS + V1_EVERY * (SLOTS - 1)
         to_reduce = {}
         to_fold = {}
 
@@ -287,13 +286,11 @@ def tile_causalselfattention2_pa_kernel(
             c = ROPE_ORDER[phase]
             ring = LAST_RING if c == LAST else RING
             new_slots = [n for n in (2 * step + 2, 2 * step + 3) if n < SLOTS]
-            v1_slot, off_beat = divmod(step - SLOTS, V1_EVERY)
+            v_chunks = V_BESIDE[phase : phase + 1]
 
             acc = project(c, j, ring)
-            if phase == 0:
-                copy_v(V0, j, ring)
-            if off_beat == 0 and 0 <= v1_slot < SLOTS:
-                copy_v(V1, v1_slot, ring)
+            for vc in v_chunks:
+                copy_v(vc, j, ring)
             if step in to_fold:
                 fold_means(to_fold[step], ring)
             for n in new_slots:
@@ -324,15 +321,13 @@ def tile_causalselfattention2_pa_kernel(
             if c == LAST and j in (4, 6):
                 add_last_pair(j // 2 - 2)
 
-            if step == v1_done:
-                store_rows(V1, 0, SLOTS)
             if j == SLOTS - 1:
                 store_means()
-                if phase == 0:
-                    store_rows(V0, 0, SLOTS)
-                store_rows(c, 0, SLOTS)
-            if c == LAST and j == SLOTS // 2 - 1:
-                store_rows(c, 0, SLOTS // 2)
+            for done in v_chunks + (c,):
+                if done in STORED_IN_HALVES and j == SLOTS // 2 - 1:
+                    store_rows(done, 0, SLOTS // 2)
+                if j == SLOTS - 1:
+                    store_rows(done, SLOTS // 2 if done in STORED_IN_HALVES else 0, SLOTS)
 
         sum_chunk, half = sums_in_step[STEPS - 1]
         sums = slot_sums(sum_chunk, half)

from contextlib import ExitStack

import concourse.mybir as mybir
from concourse.masks import make_identity

B, T, C, H, G = 2, 512, 1024, 16, 16
HS = C // H
TG = T // G
FREQS = HS // 2
FLOPS = 2 * B * T * C * 3 * C

F32 = mybir.dt.float32
BF16 = mybir.dt.bfloat16
I32 = mybir.dt.int32
U32 = mybir.dt.uint32
U8 = mybir.dt.uint8
E5M2X4 = mybir.dt.float8_e5m2_x4
E2M1X4 = mybir.dt.float4_e2m1fn_x4
ALU = mybir.AluOpType
ACT = mybir.ActivationFunctionType
AXIS_X = mybir.AxisListType.X

P = 128
SLOTS = B * T // P
PAIRS = SLOTS // 2
QUARTERS = TG // SLOTS
K_PASS = 4 * P
PASSES = C // K_PASS
NCOL = 512
CH = NCOL // HS
HALF = CH // 2
CHUNKS = 3 * C // NCOL
Q0, Q1, K0, K1, V0, V1 = range(CHUNKS)

ROPE_ORDER = (K1, Q0, Q1, K0)
STEPS = len(ROPE_ORDER) * SLOTS
LAST = ROPE_ORDER[-1]

RING, LAST_RING = 6, 4
SUM_BANK, LAST_SUM_BANK = 6, 4

V_BESIDE = (V0, V1)
SUM_ORDER = (V0, K1, V1, Q0, Q1)
SUMS_EVERY = 2
STORED_IN_HALVES = (V0, LAST)
FOLD_AFTER = 4
VECTOR_ADDS = 3
PART_BUFS = 4


def tile_causalselfattention2_pa_kernel(
    tc, x, w_attn_words, w_attn_scales, freqs_cos, freqs_sin, out_0, out_1, out_2
):
    nc = tc.nc
    outs = (out_0, out_1, out_2)

    with ExitStack() as ctx:
        keep = ctx.enter_context(tc.tile_pool(name="keep", bufs=1))
        stage = ctx.enter_context(tc.tile_pool(name="stage", bufs=3))
        psum = ctx.enter_context(tc.psum_pool(name="psum", bufs=1))
        ctx.enter_context(tc.manual_schedule())

        def bank(n):
            return psum.tile([P, NCOL], F32, name="bank%d" % n)

        x_sb = [keep.tile([P, C], BF16, name="x%d" % j) for j in range(SLOTS)]
        x_view = x.rearrange("b (m j) c -> m b j c", j=SLOTS)
        words = [keep.tile([P, PASSES, 2 * NCOL], U8, name="w%d" % c, align_bytes=64) for c in range(CHUNKS)]
        spans = ((K1, V1), (Q0, K1), (V1, CHUNKS))
        planes = [
            keep.tile([P, PASSES, (hi - lo) * NCOL], U8, name="plane%d" % lo, align_bytes=64) for lo, hi in spans
        ]

        def w_scale(c, g):
            for (lo, hi), plane in zip(spans, planes):
                if lo <= c < hi:
                    return plane[:, g, (c - lo) * NCOL : (c - lo + 1) * NCOL]

        def load_x(j):
            nc.sync.dma_start(out=x_sb[j][:], in_=x_view[:, :, j, :])

        def load_words(c):
            src = w_attn_words[:, :, 2 * NCOL * c : 2 * NCOL * (c + 1)].rearrange("g p n -> p g n")
            nc.sync.dma_start(out=words[c][:].bitcast(I32), in_=src.bitcast(I32))

        def load_scales(n):
            lo, hi = spans[n]
            for quad in range(4):
                src = w_attn_scales[:, 4 * quad : 4 * quad + 4, lo * NCOL : hi * NCOL].rearrange("g i n -> i g n")
                nc.sync.dma_start(out=planes[n][32 * quad : 32 * quad + 4, :, :].bitcast(I32), in_=src.bitcast(I32))

        for plane in planes:
            nc.vector.memset(plane[:].bitcast(I32), 0)

        load_x(0)
        cos_sb = keep.tile([P, SLOTS * FREQS], BF16)
        sin_sb = keep.tile([P, SLOTS * FREQS], BF16)
        for dst, src in ((cos_sb, freqs_cos), (sin_sb, freqs_sin)):
            by_part = src.rearrange("(m j) i -> m (j i)", j=SLOTS)
            nc.scalar.dma_start(out=dst[:], in_=by_part.unsqueeze(1).broadcast_to([P // B, B, SLOTS * FREQS]))
        load_x(1)
        load_scales(0)
        load_words(K1)
        load_words(V0)
        for j in range(2, SLOTS):
            load_x(j)
        load_scales(1)
        load_scales(2)
        for c in (Q0, V1, Q1, K0):
            load_words(c)

        ident = keep.tile([P, P], F32)
        make_identity(nc, ident[:])
        fold = keep.tile([P, HS], F32)
        nc.gpsimd.tensor_tensor(out=fold[:], in0=ident[:, 0:HS], in1=ident[:, HS:P], op=ALU.add)
        signs = keep.tile([P, 2, 2], F32)
        nc.vector.memset(signs[:], 1.0)
        nc.vector.memset(signs[:, 1, 0:1], -1.0)
        cos_tab = keep.tile([P, SLOTS * FREQS, 2], F32)
        sin_tab = keep.tile([P, SLOTS * FREQS, 2], F32)
        for n, (tab, src) in enumerate(((cos_tab, cos_sb), (sin_tab, sin_sb))):
            nc.vector.tensor_tensor(
                out=tab[:],
                in0=src[:].unsqueeze(2).broadcast_to([P, SLOTS * FREQS, 2]),
                in1=signs[:, n, :].unsqueeze(1).broadcast_to([P, SLOTS * FREQS, 2]),
                op=ALU.mult,
            )

        codes = [keep.tile([P, PASSES, P], U32, name="xc%d" % j, align_bytes=64) for j in range(SLOTS)]
        scales = [keep.tile([P, PASSES, P], U8, name="xs%d" % j, align_bytes=64) for j in range(SLOTS)]
        grouped = {}

        def transpose_x(j, passes, bank_no):
            if passes.start == 0:
                grouped[j] = stage.tile([P, C], BF16, name="grouped", align_bytes=64)
            xt = bank(bank_no)
            x_words = x_sb[j][:].bitcast(F32)
            for g in passes:
                for u in range(2):
                    col = (2 * (g - passes.start) + u) * P
                    nc.tensor.transpose(xt[:, col : col + P], x_words[:, 256 * g + u : 256 * (g + 1) : 2], ident[:])
            nc.scalar.copy(
                out=grouped[j][:, passes.start * K_PASS : passes.stop * K_PASS]
                .bitcast(F32)
                .rearrange("p (g n u) -> p g n u", g=len(passes), u=2),
                in_=xt[:, 0 : len(passes) * 2 * P].rearrange("p (g u n) -> p g n u", g=len(passes), u=2),
            )

        def quantize_x(j, passes):
            nc.vector.quantize_mx(
                out=codes[j][:, passes.start : passes.stop, :].rearrange("p g n -> p (g n)").bitcast(E5M2X4),
                scales=scales[j][:, passes.start : passes.stop, :].rearrange("p g n -> p (g n)"),
                in_=grouped[j][:, passes.start * K_PASS : passes.stop * K_PASS],
            )

        rows = [keep.tile([P, CH, SLOTS * HS], F32, name="rows%d" % c) for c in range(CHUNKS)]
        taken = []

        def next_bank(ring):
            taken.append(ring)
            return bank(len(taken) % ring)

        def project(c, j, ring):
            acc = next_bank(ring)
            for g in range(PASSES):
                nc.tensor.matmul_mx(
                    out=acc[:],
                    lhsT=codes[j][:, g, :].bitcast(E5M2X4),
                    lhsT_scale=scales[j][:, g, :],
                    rhs=words[c][:, g, :].bitcast(E2M1X4),
                    rhs_scale=w_scale(c, g),
                    start=(g == 0),
                    stop=(g == PASSES - 1),
                )
            return acc

        def rope_products(acc, j, cos_part, sin_part, heads):
            place = slice((j % 2) * HS, (j % 2 + 1) * HS)
            freq = slice(j * FREQS, (j + 1) * FREQS)
            shape = [P, heads.stop - heads.start, FREQS, 2]
            pairs = acc[:].rearrange("p (h i e) -> p h i e", h=CH, e=2)[:, heads]
            nc.vector.tensor_tensor(
                out=cos_part[:, heads, place].rearrange("p h (i e) -> p h i e", e=2),
                in0=cos_tab[:, freq, :].unsqueeze(1).broadcast_to(shape),
                in1=pairs,
                op=ALU.mult,
            )
            nc.vector.tensor_tensor(
                out=sin_part[:, heads, place].rearrange("p h (i e) -> p h i e", e=2),
                in0=sin_tab[:, freq, :].unsqueeze(1).broadcast_to(shape),
                in1=pairs[:, :, :, ::-1],
                op=ALU.mult,
            )

        def rope_add(engine, c, cos_part, sin_part, j_lo, j_hi, heads):
            place = slice((j_lo % 2) * HS, ((j_hi - 1) % 2 + 1) * HS)
            engine.tensor_tensor(
                out=rows[c][:, heads, j_lo * HS : j_hi * HS],
                in0=cos_part[:, heads, place],
                in1=sin_part[:, heads, place],
                op=ALU.add,
            )

        def copy_v(c, j, ring):
            acc = project(c, j, ring)
            nc.scalar.copy(out=rows[c][:, :, j * HS : (j + 1) * HS], in_=acc[:].rearrange("p (h d) -> p h d", h=CH))

        def store_rows(c, j_lo, j_hi):
            for h in range(CH):
                for b in range(B):
                    dst = outs[c // 2][b, (c % 2) * CH + h, :, 0:TG, :].rearrange("g (r j) d -> g r (j d)", j=SLOTS)
                    nc.sync.dma_start(
                        out=dst[:, :, j_lo * HS : j_hi * HS], in_=rows[c][b:P:B, h, j_lo * HS : j_hi * HS]
                    )

        group_sums = {c: keep.tile([P, B, CH * G], F32, name="gs%d" % c) for c in SUM_ORDER + (LAST,)}
        waiting_means = []

        def add_transposed(sums, c, h, u, start, stop):
            nc.tensor.matmul(
                out=sums[:, (h % HALF) * P : (h % HALF + 1) * P],
                lhsT=rows[c][:, h, u * P : (u + 1) * P],
                rhs=ident[:],
                start=start,
                stop=stop,
                is_transpose=True,
            )

        def slot_sums(c, half):
            sums = bank(SUM_BANK + half)
            for h in range(HALF * half, HALF * (half + 1)):
                for u in range(PAIRS):
                    add_transposed(sums, c, h, u, u == 0, u == PAIRS - 1)
            return sums

        last_sums = []

        def add_last_pair(u):
            if u == 0:
                last_sums.extend((bank(LAST_SUM_BANK), bank(LAST_SUM_BANK + 1)))
            for h in range(CH):
                first = u == 0 and h % HALF == 0
                final = u == PAIRS - 1 and h % HALF == HALF - 1
                add_transposed(last_sums[h // HALF], LAST, h, u, first, final)

        def reduce_quarters(sums, c, half):
            dst = group_sums[c][:, :, half * HALF * G : (half + 1) * HALF * G]
            nc.vector.tensor_reduce(
                out=dst, in_=sums[:].rearrange("p (n r b) -> p b n r", r=QUARTERS, b=B), axis=AXIS_X, op=ALU.add
            )

        def fold_means(c, ring):
            acc = next_bank(ring)
            for b in range(B):
                nc.tensor.matmul(
                    out=acc[:, b * HS : (b + 1) * HS], lhsT=group_sums[c][:, b, :], rhs=fold[:], start=True, stop=True
                )
            means = keep.tile([P, B, HS], F32, name="means%d" % c)
            nc.scalar.activation(
                out=means[:], in_=acc[:, 0 : B * HS].rearrange("p (b d) -> p b d", b=B), func=ACT.Copy, scale=1.0 / TG
            )
            dst = outs[c // 2][:, (c % 2) * CH : (c % 2 + 1) * CH, :, TG, :].rearrange("b h g d -> (h g) b d")
            waiting_means.append((dst, means[:]))

        def store_means():
            for dst, src in waiting_means:
                nc.sync.dma_start(out=dst, in_=src)
            waiting_means.clear()

        all_passes = range(PASSES)
        all_heads = slice(0, CH)
        halves = [slice(HALF * half, HALF * (half + 1)) for half in range(2)]
        sum_steps = range(STEPS - 1 - SUMS_EVERY * (2 * len(SUM_ORDER) - 1), STEPS, SUMS_EVERY)
        sums_in_step = {step: (SUM_ORDER[n // 2], n % 2) for n, step in enumerate(sum_steps)}
        to_reduce = {}
        to_fold = {}

        for g in all_passes:
            transpose_x(0, range(g, g + 1), SUM_BANK + g)
            quantize_x(0, range(g, g + 1))
        transpose_x(1, all_passes, RING - 1)
        quantize_x(1, all_passes)

        for step in range(STEPS):
            phase, j = divmod(step, SLOTS)
            c = ROPE_ORDER[phase]
            ring = LAST_RING if c == LAST else RING
            new_slots = [n for n in (2 * step + 2, 2 * step + 3) if n < SLOTS]
            v_chunks = V_BESIDE[phase : phase + 1]

            acc = project(c, j, ring)
            for vc in v_chunks:
                copy_v(vc, j, ring)
            if step in to_fold:
                fold_means(to_fold[step], ring)
            for n in new_slots:
                transpose_x(n, all_passes, SUM_BANK + n % 2)
            if j % 2 == 0:
                cos_part = stage.tile([P, CH, 2 * HS], F32, name="cos_part", bufs=PART_BUFS)
                sin_part = stage.tile([P, CH, 2 * HS], F32, name="sin_part", bufs=PART_BUFS)
            if step == STEPS - 1:
                break

            rope_products(acc, j, cos_part, sin_part, all_heads)
            for n in new_slots:
                quantize_x(n, all_passes)
            if step in to_reduce:
                reduce_quarters(*to_reduce[step])
            if step < VECTOR_ADDS:
                rope_add(nc.vector, c, cos_part, sin_part, j, j + 1, all_heads)
            elif step in (VECTOR_ADDS, STEPS - 2):
                rope_add(nc.gpsimd, c, cos_part, sin_part, j, j + 1, all_heads)
            elif j % 2 == 1:
                rope_add(nc.gpsimd, c, cos_part, sin_part, j - 1, j + 1, all_heads)

            if step in sums_in_step:
                sum_chunk, half = sums_in_step[step]
                to_reduce[step + 1] = (slot_sums(sum_chunk, half), sum_chunk, half)
                if half == 1:
                    to_fold[step + FOLD_AFTER] = sum_chunk
            if c == LAST and j in (4, 6):
                add_last_pair(j // 2 - 2)

            if j == SLOTS - 1:
                store_means()
            for done in v_chunks + (c,):
                if done in STORED_IN_HALVES and j == SLOTS // 2 - 1:
                    store_rows(done, 0, SLOTS // 2)
                if j == SLOTS - 1:
                    store_rows(done, SLOTS // 2 if done in STORED_IN_HALVES else 0, SLOTS)

        sum_chunk, half = sums_in_step[STEPS - 1]
        sums = slot_sums(sum_chunk, half)
        add_last_pair(PAIRS - 2)
        for heads in halves:
            rope_products(acc, j, cos_part, sin_part, heads)
        for heads in halves:
            rope_add(nc.vector, LAST, cos_part, sin_part, j, j + 1, heads)
        store_means()
        store_rows(LAST, SLOTS // 2, SLOTS)
        reduce_quarters(sums, sum_chunk, half)
        add_last_pair(PAIRS - 1)
        fold_means(sum_chunk, LAST_RING)
        for half in range(2):
            reduce_quarters(last_sums[half], LAST, half)
        fold_means(LAST, LAST_RING)
        store_means()
